import numpy as np
import ml_dtypes


def mxq(x, axis, fmt="e4m3"):
    dtype, down = {"e4m3": (ml_dtypes.float8_e4m3fn, 7), "e5m2": (ml_dtypes.float8_e5m2, 14)}[fmt]
    v = np.moveaxis(np.asarray(x, np.float32).astype(ml_dtypes.bfloat16).astype(np.float64), axis, -1)
    blocks = v.reshape(v.shape[:-1] + (-1, 32))
    amax = np.abs(blocks).max(-1, keepdims=True)
    byte = np.maximum(np.where(amax > 0, np.frexp(amax)[1] - 1 + 127, 0) - down, 1)
    scale = np.exp2(byte - 127.0)
    codes = (blocks / scale).astype(np.float32).astype(dtype).astype(np.float64)
    return np.moveaxis((codes * scale).reshape(v.shape), -1, axis)


WIDE = False


def mx_kscale(k):
    if not WIDE:
        return np.ones(k)
    levels = np.array([10, -10, 5, -5, 0])
    a = np.random.permutation(np.resize(levels, k // 512 * 4)).reshape(k // 512, 4)
    idx = np.arange(k)
    return np.exp2(a[idx // 512, idx % 128 // 32])


BF16 = ml_dtypes.bfloat16


def bf(x):
    return np.asarray(x, np.float32).astype(BF16)


def f64(x):
    return np.asarray(x).astype(np.float64)


B, NV, S, D, H = 2, 8, 512, 512, 8
HD = D // H


def setup_inputs():
    s, t = mx_kscale(D), mx_kscale(D)
    return {"x": bf(np.random.standard_normal((B * NV, S, D)) * s),
            "scores": bf(np.random.standard_normal((B, NV, NV, H, S)) * 1.4),
            "Wv": bf(np.random.standard_normal((D, D)) / np.sqrt(D) / s[:, None] * t),
            "bv": bf(np.random.standard_normal(D) * 0.3 * t),
            "Wo": bf(np.random.standard_normal((D, D)) / np.sqrt(D) / t[:, None]),
            "bo": bf(np.random.standard_normal(D) * 0.3)}


def reference(x, scores, Wv, bv, Wo, bo):
    v = (mxq(f64(x), 2, "e4m3") @ mxq(f64(Wv), 0, "e4m3")) + f64(bv)
    v = v.reshape(B, NV, S, H, HD).transpose(0, 1, 3, 2, 4)
    sc = f64(scores)
    e = np.exp(sc - sc.max(2, keepdims=True))
    w = e / e.sum(2, keepdims=True)
    mixed = np.zeros((B, NV, H, S, HD))
    for j in range(NV):
        mixed = mixed + w[:, :, j, :, :, None] * v[:, j][:, None]
    mixed = mixed.transpose(0, 1, 3, 2, 4).reshape(B * NV, S, D)
    return (mxq(mixed, 2, "e4m3") @ mxq(f64(Wo), 0, "e4m3")) + f64(bo)

@@ -1,0 +1,225 @@
+from contextlib import ExitStack
+
+import concourse.mybir as mybir
+from concourse.masks import make_identity
+
+F32 = mybir.dt.float32
+BF16 = mybir.dt.bfloat16
+U32 = mybir.dt.uint32
+U8 = mybir.dt.uint8
+FP8X4 = mybir.dt.float8_e4m3fn_x4
+ALU = mybir.AluOpType
+ACT = mybir.ActivationFunctionType
+
+P = 128
+PACK = 4
+B = 2
+NV = 8
+S = 512
+D = 512
+H = 8
+HD = D // H
+T = P // NV
+G = S // T
+OCT = 8
+N_OCT = G // OCT
+STORE = 4
+
+FLOPS = 2 * 2 * B * NV * S * D * D + 2 * B * NV * NV * S * D
+
+
+def quantise_weight(nc, setup, keep, name, load_rows):
+    raw = setup.tile([P, PACK, D], BF16, name=name + "_raw")
+    load_rows(raw)
+    grouped = setup.tile([P, D, PACK], BF16, name=name + "_grouped", align_bytes=64)
+    nc.vector.tensor_copy(out=grouped[:], in_=raw[:].rearrange("p a c -> p c a"))
+    codes = keep.tile([P, D], U32, name=name + "_codes", align_bytes=64)
+    scales = keep.tile([P, D], U8, name=name + "_scales", align_bytes=64)
+    nc.vector.quantize_mx(
+        out=codes[:].bitcast(FP8X4), scales=scales[:], in_=grouped[:].rearrange("p c a -> p (c a)")
+    )
+    return codes, scales
+
+
+def softmax_over_views(nc, setup, scores):
+    raw = setup.tile([P, NV, S], BF16, name="scores_raw")
+    for h in range(H):
+        nc.scalar.dma_start(
+            out=raw[h * B * NV : (h + 1) * B * NV, :, :],
+            in_=scores[:, :, :, h, :].rearrange("b i j s -> (b i) j s"),
+        )
+    top = setup.tile([P, NV // 2, S], BF16, name="scores_top")
+    nc.vector.tensor_max(out=top[:], in0=raw[:, 0:4, :], in1=raw[:, 4:8, :])
+    nc.vector.tensor_max(out=top[:, 0:2, :], in0=top[:, 0:2, :], in1=top[:, 2:4, :])
+    nc.vector.tensor_max(out=top[:, 0:1, :], in0=top[:, 0:1, :], in1=top[:, 1:2, :])
+    e = setup.tile([P, NV, S], F32, name="scores_exp")
+    nc.vector.tensor_tensor(
+        out=e[:], in0=raw[:], in1=top[:, 0:1, :].to_broadcast([P, NV, S]), op=ALU.subtract
+    )
+    nc.scalar.activation(out=e[:], in_=e[:], func=ACT.Exp)
+    total = setup.tile([P, NV // 2, S], F32, name="scores_total")
+    nc.vector.tensor_add(out=total[:], in0=e[:, 0:4, :], in1=e[:, 4:8, :])
+    nc.vector.tensor_add(out=total[:, 0:2, :], in0=total[:, 0:2, :], in1=total[:, 2:4, :])
+    nc.vector.tensor_add(out=total[:, 0:1, :], in0=total[:, 0:1, :], in1=total[:, 1:2, :])
+    nc.vector.reciprocal(out=total[:, 0:1, :], in_=total[:, 0:1, :])
+    w = setup.tile([P, N_OCT, NV, OCT, T], F32, name="softmax_w")
+    e_sorted = e[:].rearrange("p j (t o r) -> p o j r t", t=T, o=N_OCT, r=OCT)
+    inv_sorted = total[:, 0:1, :].rearrange("p j (t o r) -> p o j r t", t=T, o=N_OCT, r=OCT)
+    for o in range(N_OCT):
+        nc.vector.tensor_tensor(
+            out=w[:, o, :, :, :],
+            in0=e_sorted[:, o, :, :, :],
+            in1=inv_sorted[:, o, :, :, :].to_broadcast([P, NV, OCT, T]),
+            op=ALU.mult,
+        )
+    return w
+
+
+def tile_crossviewattention_pa_t_kernel(tc, x, scores, Wv, bv, Wo, bo, out):
+    nc = tc.nc
+    x_tiles = x.flatten_outer_dims().rearrange("(b p g) d -> b p g d", b=B, p=P, g=G)
+    out_tiles = out.flatten_outer_dims().rearrange("(b p g) d -> b p g d", b=B, p=P, g=G)
+
+    with ExitStack() as stack:
+        keep = stack.enter_context(tc.tile_pool(name="keep", bufs=1))
+        setup = stack.enter_context(tc.tile_pool(name="setup", bufs=1))
+        stream = stack.enter_context(tc.tile_pool(name="stream", bufs=2))
+        sums = stack.enter_context(tc.tile_pool(name="sums", bufs=1))
+        results = stack.enter_context(tc.tile_pool(name="results", bufs=3))
+        ps_words = stack.enter_context(tc.psum_pool(name="ps_words", bufs=2))
+        ps_v = stack.enter_context(tc.psum_pool(name="ps_v", bufs=2))
+        ps_mixed = stack.enter_context(tc.psum_pool(name="ps_mixed", bufs=2))
+        ps_y = stack.enter_context(tc.psum_pool(name="ps_y", bufs=2))
+
+        ident_f32 = keep.tile([P, P], F32, name="ident_f32")
+        make_identity(nc, ident_f32[:])
+        ident_bf16 = keep.tile([P, P], BF16, name="ident_bf16")
+        make_identity(nc, ident_bf16[:])
+        bv_all = keep.tile([P, D], BF16, name="bv_all")
+        nc.scalar.dma_start(out=bv_all[:], in_=bv.partition_broadcast(P))
+        bo_all = keep.tile([P, D], BF16, name="bo_all")
+        nc.scalar.dma_start(out=bo_all[:], in_=bo.partition_broadcast(P))
+
+        def load_wv(raw):
+            for u in range(2):
+                nc.scalar.dma_start(
+                    out=raw[:, 2 * u : 2 * u + 2, :],
+                    in_=Wv[256 * u : 256 * (u + 1), :].rearrange("(q e) c -> q e c", e=2),
+                )
+
+        def load_wo(raw):
+            nc.scalar.dma_start(out=raw[:], in_=Wo.rearrange("(a p) c -> p a c", p=P))
+
+        wv_codes, wv_scales = quantise_weight(nc, setup, keep, "wv", load_wv)
+        wo_codes, wo_scales = quantise_weight(nc, setup, keep, "wo", load_wo)
+
+        w = softmax_over_views(nc, setup, scores)
+        w_cols = keep.tile([P, N_OCT, NV, P], F32, name="w_cols")
+        for o in range(N_OCT):
+            for j0 in range(0, NV, 4):
+                wt = ps_words.tile([P, 4, P], F32, tag="words", name="wt")
+                for k in range(4):
+                    nc.tensor.transpose(
+                        out=wt[:, k, :],
+                        in_=w[:, o, j0 + k, :, :].rearrange("p r t -> p (r t)"),
+                        identity=ident_f32[:],
+                    )
+                nc.vector.tensor_copy(out=w_cols[:, o, j0 : j0 + 4, :], in_=wt[:])
+
+        for b in range(B):
+            for o in range(N_OCT):
+                x_oct = stream.tile([P, OCT * D], BF16, name="x_oct")
+                nc.sync.dma_start(
+                    out=x_oct[:],
+                    in_=x_tiles[b, :, o * OCT : (o + 1) * OCT, :].rearrange("p r d -> p (r d)"),
+                )
+                x_words = x_oct[:].bitcast(F32)
+                xg = stream.tile([P, NV * P * PACK], BF16, name="xg", align_bytes=64)
+                xg_words = xg[:].bitcast(F32).rearrange(
+                    "p (j r t u) -> p j r t u", j=NV, r=OCT, t=T, u=2
+                )
+                for r0 in range(0, OCT, 2):
+                    xt = ps_words.tile([P, 2, 2, P], F32, tag="words", name="xt")
+                    for k in range(2):
+                        for u in range(2):
+                            first = (r0 + k) * (D // 2) + u * P
+                            nc.tensor.transpose(
+                                out=xt[:, k, u, :],
+                                in_=x_words[:, first : first + P],
+                                identity=ident_f32[:],
+                            )
+                    for k in range(2):
+                        nc.scalar.copy(
+                            out=xg_words[:, :, r0 + k, :, :],
+                            in_=xt[:, k, :, :].rearrange("p u (j t) -> p j t u", j=NV, t=T),
+                        )
+                x_codes = stream.tile([P, NV * P], U32, name="x_codes", align_bytes=64)
+                x_scales = stream.tile([P, NV * P], U8, name="x_scales", align_bytes=64)
+                nc.vector.quantize_mx(out=x_codes[:].bitcast(FP8X4), scales=x_scales[:], in_=xg[:])
+
+                acc = sums.tile([P, NV, D], F32, name="acc")
+                mixed = stream.tile([P, NV, D], BF16, name="mixed")
+                for j in range(NV):
+                    tokens = slice(j * P, (j + 1) * P)
+                    v = ps_v.tile([P, D], F32, name="v")
+                    nc.tensor.matmul_mx(
+                        out=v[:],
+                        lhsT=x_codes[:, tokens].bitcast(FP8X4),
+                        lhsT_scale=x_scales[:, tokens],
+                        rhs=wv_codes[:].bitcast(FP8X4),
+                        rhs_scale=wv_scales[:],
+                        start=True,
+                        stop=True,
+                    )
+                    for i in range(NV):
+                        for h in range(H):
+                            head = slice(h * HD, (h + 1) * HD)
+                            col = (h * B + b) * NV + i
+                            before = bv_all[:, head] if j == 0 else acc[:, i, head]
+                            after = mixed[:, i, head] if j == NV - 1 else acc[:, i, head]
+                            nc.vector.scalar_tensor_tensor(
+                                out=after,
+                                in0=v[:, head],
+                                scalar=w_cols[:, o, j, col : col + 1],
+                                in1=before,
+                                op0=ALU.mult,
+                                op1=ALU.add,
+                            )
+
+                mg = stream.tile([P, OCT * P * PACK], BF16, name="mg", align_bytes=64)
+                mg_tiles = mg[:].rearrange("p (r i t a) -> p r i t a", r=OCT, i=NV, t=T, a=PACK)
+                for i0 in range(0, NV, 2):
+                    mt = ps_mixed.tile([P, 2, PACK, P], BF16, name="mt")
+                    for k in range(2):
+                        for a in range(PACK):
+                            nc.tensor.transpose(
+                                out=mt[:, k, a, :],
+                                in_=mixed[:, i0 + k, a * P : (a + 1) * P],
+                                identity=ident_bf16[:],
+                            )
+                    for k in range(2):
+                        nc.scalar.copy(
+                            out=mg_tiles[:, :, i0 + k, :, :],
+                            in_=mt[:, k, :, :].rearrange("p a (r t) -> p r t a", r=OCT, t=T),
+                        )
+                m_codes = stream.tile([P, OCT * P], U32, name="m_codes", align_bytes=64)
+                m_scales = stream.tile([P, OCT * P], U8, name="m_scales", align_bytes=64)
+                nc.vector.quantize_mx(out=m_codes[:].bitcast(FP8X4), scales=m_scales[:], in_=mg[:])
+
+                for r0 in range(0, OCT, STORE):
+                    y_sb = results.tile([P, STORE, D], F32, name="y_sb")
+                    for k in range(STORE):
+                        tokens = slice((r0 + k) * P, (r0 + k + 1) * P)
+                        y = ps_y.tile([P, D], F32, name="y")
+                        nc.tensor.matmul_mx(
+                            out=y[:],
+                            lhsT=m_codes[:, tokens].bitcast(FP8X4),
+                            lhsT_scale=m_scales[:, tokens],
+                            rhs=wo_codes[:].bitcast(FP8X4),
+                            rhs_scale=wo_scales[:],
+                            start=True,
+                            stop=True,
+                        )
+                        nc.vector.tensor_tensor(out=y_sb[:, k, :], in0=y[:], in1=bo_all[:], op=ALU.add)
+                    g0 = o * OCT + r0
+                    nc.sync.dma_start(out=out_tiles[b, :, g0 : g0 + STORE, :], in_=y_sb[:])

@@ -23,15 +23,20 @@ T = P // NV
 G = S // T
 OCT = 8
 N_OCT = G // OCT
-STORE = 4
+VEC_OCT = N_OCT - 1
+TENSOR_TILES = VEC_OCT * OCT
+QUAD = 4
+STORE = 2
+UNITS = 3
+HEAD_START = NV
 
 FLOPS = 2 * 2 * B * NV * S * D * D + 2 * B * NV * NV * S * D
 
 
 def quantise_weight(nc, setup, keep, name, load_rows):
-    raw = setup.tile([P, PACK, D], BF16, name=name + "_raw")
+    raw = setup.tile([P, PACK, D], BF16, name="w_raw")
     load_rows(raw)
-    grouped = setup.tile([P, D, PACK], BF16, name=name + "_grouped", align_bytes=64)
+    grouped = setup.tile([P, D, PACK], BF16, name="w_grouped", align_bytes=64)
     nc.vector.tensor_copy(out=grouped[:], in_=raw[:].rearrange("p a c -> p c a"))
     codes = keep.tile([P, D], U32, name=name + "_codes", align_bytes=64)
     scales = keep.tile([P, D], U8, name=name + "_scales", align_bytes=64)
@@ -41,37 +46,43 @@ def quantise_weight(nc, setup, keep, name, load_rows):
     return codes, scales
 
 
-def softmax_over_views(nc, setup, scores):
+def load_scores(nc, setup, scores):
     raw = setup.tile([P, NV, S], BF16, name="scores_raw")
     for h in range(H):
         nc.scalar.dma_start(
             out=raw[h * B * NV : (h + 1) * B * NV, :, :],
             in_=scores[:, :, :, h, :].rearrange("b i j s -> (b i) j s"),
         )
-    top = setup.tile([P, NV // 2, S], BF16, name="scores_top")
-    nc.vector.tensor_max(out=top[:], in0=raw[:, 0:4, :], in1=raw[:, 4:8, :])
-    nc.vector.tensor_max(out=top[:, 0:2, :], in0=top[:, 0:2, :], in1=top[:, 2:4, :])
-    nc.vector.tensor_max(out=top[:, 0:1, :], in0=top[:, 0:1, :], in1=top[:, 1:2, :])
-    e = setup.tile([P, NV, S], F32, name="scores_exp")
+    return raw
+
+
+def softmax_exponentials(nc, soft, raw, o):
+    part = raw[:].rearrange("p j (t o r) -> p o j t r", t=T, o=N_OCT, r=OCT)[:, o, :, :, :]
+    top = soft.tile([P, NV // 2, T, OCT], BF16, name="top")
+    nc.vector.tensor_max(out=top[:], in0=part[:, 0:4, :, :], in1=part[:, 4:8, :, :])
+    nc.vector.tensor_max(out=top[:, 0:2, :, :], in0=top[:, 0:2, :, :], in1=top[:, 2:4, :, :])
+    nc.vector.tensor_max(out=top[:, 0:1, :, :], in0=top[:, 0:1, :, :], in1=top[:, 1:2, :, :])
+    e = soft.tile([P, NV, T, OCT], F32, name="e")
     nc.vector.tensor_tensor(
-        out=e[:], in0=raw[:], in1=top[:, 0:1, :].to_broadcast([P, NV, S]), op=ALU.subtract
+        out=e[:], in0=part, in1=top[:, 0:1, :, :].to_broadcast([P, NV, T, OCT]), op=ALU.subtract
     )
     nc.scalar.activation(out=e[:], in_=e[:], func=ACT.Exp)
-    total = setup.tile([P, NV // 2, S], F32, name="scores_total")
-    nc.vector.tensor_add(out=total[:], in0=e[:, 0:4, :], in1=e[:, 4:8, :])
-    nc.vector.tensor_add(out=total[:, 0:2, :], in0=total[:, 0:2, :], in1=total[:, 2:4, :])
-    nc.vector.tensor_add(out=total[:, 0:1, :], in0=total[:, 0:1, :], in1=total[:, 1:2, :])
-    nc.vector.reciprocal(out=total[:, 0:1, :], in_=total[:, 0:1, :])
-    w = setup.tile([P, N_OCT, NV, OCT, T], F32, name="softmax_w")
-    e_sorted = e[:].rearrange("p j (t o r) -> p o j r t", t=T, o=N_OCT, r=OCT)
-    inv_sorted = total[:, 0:1, :].rearrange("p j (t o r) -> p o j r t", t=T, o=N_OCT, r=OCT)
-    for o in range(N_OCT):
-        nc.vector.tensor_tensor(
-            out=w[:, o, :, :, :],
-            in0=e_sorted[:, o, :, :, :],
-            in1=inv_sorted[:, o, :, :, :].to_broadcast([P, NV, OCT, T]),
-            op=ALU.mult,
-        )
+    return e
+
+
+def softmax_weights(nc, soft, e, order, shape):
+    total = soft.tile([P, NV // 2, T, OCT], F32, name="total")
+    nc.vector.tensor_add(out=total[:], in0=e[:, 0:4, :, :], in1=e[:, 4:8, :, :])
+    nc.vector.tensor_add(out=total[:, 0:2, :, :], in0=total[:, 0:2, :, :], in1=total[:, 2:4, :, :])
+    nc.vector.tensor_add(out=total[:, 0:1, :, :], in0=total[:, 0:1, :, :], in1=total[:, 1:2, :, :])
+    nc.vector.reciprocal(out=total[:, 0:1, :, :], in_=total[:, 0:1, :, :])
+    w = soft.tile([P] + shape, F32, name="w")
+    nc.vector.tensor_tensor(
+        out=w[:],
+        in0=e[:].rearrange("p j t r -> p " + order),
+        in1=total[:, 0:1, :, :].rearrange("p j t r -> p " + order).to_broadcast([P] + shape),
+        op=ALU.mult,
+    )
     return w
 
 
@@ -83,22 +94,76 @@ def tile_crossviewattention_pa_t_kernel(tc, x, scores, Wv, bv, Wo, bo, out):
     with ExitStack() as stack:
         keep = stack.enter_context(tc.tile_pool(name="keep", bufs=1))
         setup = stack.enter_context(tc.tile_pool(name="setup", bufs=1))
-        stream = stack.enter_context(tc.tile_pool(name="stream", bufs=2))
-        sums = stack.enter_context(tc.tile_pool(name="sums", bufs=1))
-        results = stack.enter_context(tc.tile_pool(name="results", bufs=3))
-        ps_words = stack.enter_context(tc.psum_pool(name="ps_words", bufs=2))
-        ps_v = stack.enter_context(tc.psum_pool(name="ps_v", bufs=2))
-        ps_mixed = stack.enter_context(tc.psum_pool(name="ps_mixed", bufs=2))
-        ps_y = stack.enter_context(tc.psum_pool(name="ps_y", bufs=2))
+        soft = stack.enter_context(tc.tile_pool(name="soft", bufs=2))
+        two = stack.enter_context(tc.tile_pool(name="two", bufs=2))
+        three = stack.enter_context(tc.tile_pool(name="three", bufs=3))
+        four = stack.enter_context(tc.tile_pool(name="four", bufs=4))
+        ps_view = stack.enter_context(tc.psum_pool(name="ps_view", bufs=2))
+        ps_v = stack.enter_context(tc.psum_pool(name="ps_v", bufs=1))
+        ps_mix = stack.enter_context(tc.psum_pool(name="ps_mix", bufs=2))
+        ps_y = stack.enter_context(tc.psum_pool(name="ps_y", bufs=1))
+        ps_turn = stack.enter_context(tc.psum_pool(name="ps_turn", bufs=2))
+        stack.enter_context(tc.manual_schedule())
 
         ident_f32 = keep.tile([P, P], F32, name="ident_f32")
         make_identity(nc, ident_f32[:])
         ident_bf16 = keep.tile([P, P], BF16, name="ident_bf16")
         make_identity(nc, ident_bf16[:])
-        bv_all = keep.tile([P, D], BF16, name="bv_all")
-        nc.scalar.dma_start(out=bv_all[:], in_=bv.partition_broadcast(P))
-        bo_all = keep.tile([P, D], BF16, name="bo_all")
-        nc.scalar.dma_start(out=bo_all[:], in_=bo.partition_broadcast(P))
+        same_t = keep.tile([P, T], F32, name="same_t")
+        nc.vector.tensor_reduce(
+            out=same_t[:],
+            in_=ident_f32[:].rearrange("p (j t) -> p t j", j=NV, t=T),
+            axis=mybir.AxisListType.X,
+            op=ALU.add,
+        )
+
+        octet_order = [0, VEC_OCT] + list(range(1, VEC_OCT))
+        x_order = [(b, o) for b in range(B) for o in octet_order]
+        x_loaded = {}
+        x_mx = {}
+
+        def load_x(n):
+            b, o = x_order[n]
+            x_oct = two.tile([P, OCT * D], BF16, name="x_oct")
+            nc.sync.dma_start(
+                out=x_oct[:],
+                in_=x_tiles[b, :, o * OCT : (o + 1) * OCT, :].rearrange("p r d -> p (r d)"),
+            )
+            x_loaded[n] = x_oct
+
+        def prepare_x(n):
+            b, o = x_order[n]
+            x_words = x_loaded[n][:].bitcast(F32)
+            xg = keep.tile([P, OCT * P * PACK], BF16, name="xg", align_bytes=64)
+            xg_words = xg[:].bitcast(F32)
+            by_tile = xg_words.rearrange("p (r n u) -> p r n u", r=OCT, n=P, u=2)
+            by_view = xg_words.rearrange("p (j r t u) -> p j r t u", j=NV, r=OCT, t=T, u=2)
+            for r0 in range(0, OCT, 2):
+                xt = ps_turn.tile([P, 2, 2, P], F32, tag="turn", name="xt")
+                for k in range(2):
+                    for u in range(2):
+                        first = (r0 + k) * (D // 2) + u * P
+                        nc.tensor.transpose(
+                            out=xt[:, k, u, :], in_=x_words[:, first : first + P], identity=ident_f32[:]
+                        )
+                if o == VEC_OCT:
+                    for k in range(2):
+                        nc.scalar.copy(
+                            out=by_view[:, :, r0 + k, :, :],
+                            in_=xt[:, k, :, :].rearrange("p u (j t) -> p j t u", j=NV, t=T),
+                        )
+                else:
+                    nc.scalar.copy(
+                        out=by_tile[:, r0 : r0 + 2, :, :], in_=xt[:].rearrange("p k u n -> p k n u")
+                    )
+            pool = two if o == VEC_OCT else four
+            kind = "view" if o == VEC_OCT else "tile"
+            codes = pool.tile([P, OCT * P], U32, name="x_codes_" + kind, align_bytes=64)
+            scales = pool.tile([P, OCT * P], U8, name="x_scales_" + kind, align_bytes=64)
+            nc.vector.quantize_mx(out=codes[:].bitcast(FP8X4), scales=scales[:], in_=xg[:])
+            x_mx[(b, o)] = (codes, scales)
+            if n + 2 < len(x_order):
+                load_x(n + 2)
 
         def load_wv(raw):
             for u in range(2):
@@ -110,116 +175,251 @@ def tile_crossviewattention_pa_t_kernel(tc, x, scores, Wv, bv, Wo, bo, out):
         def load_wo(raw):
             nc.scalar.dma_start(out=raw[:], in_=Wo.rearrange("(a p) c -> p a c", p=P))
 
-        wv_codes, wv_scales = quantise_weight(nc, setup, keep, "wv", load_wv)
-        wo_codes, wo_scales = quantise_weight(nc, setup, keep, "wo", load_wo)
+        w_rows = keep.tile([P, TENSOR_TILES, P], F32, name="w_rows")
+        w_cols = keep.tile([P, NV, P], F32, name="w_cols")
+        w_by_scene = w_rows[:].rearrange("p g (h b i) -> p b g h i", h=H, b=B, i=NV)
 
-        w = softmax_over_views(nc, setup, scores)
-        w_cols = keep.tile([P, N_OCT, NV, P], F32, name="w_cols")
-        for o in range(N_OCT):
-            for j0 in range(0, NV, 4):
-                wt = ps_words.tile([P, 4, P], F32, tag="words", name="wt")
+        def spread_weights(o, e):
+            if o == VEC_OCT:
+                w = softmax_weights(nc, soft, e, "j r t", [NV, OCT, T])
+                turned = w_cols
+            else:
+                w = softmax_weights(nc, soft, e, "r j t", [OCT, NV, T])
+                turned = w_rows[:, o * OCT : (o + 1) * OCT, :]
+            for first in range(0, OCT, 4):
+                wt = ps_turn.tile([P, 4, P], F32, tag="turn", name="wt")
                 for k in range(4):
                     nc.tensor.transpose(
                         out=wt[:, k, :],
-                        in_=w[:, o, j0 + k, :, :].rearrange("p r t -> p (r t)"),
+                        in_=w[:, first + k, :, :].rearrange("p m n -> p (m n)"),
                         identity=ident_f32[:],
                     )
-                nc.vector.tensor_copy(out=w_cols[:, o, j0 : j0 + 4, :], in_=wt[:])
+                nc.scalar.copy(out=turned[:, first : first + 4, :], in_=wt[:])
 
-        for b in range(B):
-            for o in range(N_OCT):
-                x_oct = stream.tile([P, OCT * D], BF16, name="x_oct")
-                nc.sync.dma_start(
-                    out=x_oct[:],
-                    in_=x_tiles[b, :, o * OCT : (o + 1) * OCT, :].rearrange("p r d -> p (r d)"),
-                )
-                x_words = x_oct[:].bitcast(F32)
-                xg = stream.tile([P, NV * P * PACK], BF16, name="xg", align_bytes=64)
-                xg_words = xg[:].bitcast(F32).rearrange(
-                    "p (j r t u) -> p j r t u", j=NV, r=OCT, t=T, u=2
-                )
-                for r0 in range(0, OCT, 2):
-                    xt = ps_words.tile([P, 2, 2, P], F32, tag="words", name="xt")
-                    for k in range(2):
-                        for u in range(2):
-                            first = (r0 + k) * (D // 2) + u * P
-                            nc.tensor.transpose(
-                                out=xt[:, k, u, :],
-                                in_=x_words[:, first : first + P],
-                                identity=ident_f32[:],
-                            )
-                    for k in range(2):
-                        nc.scalar.copy(
-                            out=xg_words[:, :, r0 + k, :, :],
-                            in_=xt[:, k, :, :].rearrange("p u (j t) -> p j t u", j=NV, t=T),
-                        )
-                x_codes = stream.tile([P, NV * P], U32, name="x_codes", align_bytes=64)
-                x_scales = stream.tile([P, NV * P], U8, name="x_scales", align_bytes=64)
-                nc.vector.quantize_mx(out=x_codes[:].bitcast(FP8X4), scales=x_scales[:], in_=xg[:])
+        mixers = stack.enter_context(tc.tile_pool(name="mixers", bufs=3))
+        mixer_of = {}
 
-                acc = sums.tile([P, NV, D], F32, name="acc")
-                mixed = stream.tile([P, NV, D], BF16, name="mixed")
-                for j in range(NV):
-                    tokens = slice(j * P, (j + 1) * P)
-                    v = ps_v.tile([P, D], F32, name="v")
-                    nc.tensor.matmul_mx(
-                        out=v[:],
-                        lhsT=x_codes[:, tokens].bitcast(FP8X4),
-                        lhsT_scale=x_scales[:, tokens],
-                        rhs=wv_codes[:].bitcast(FP8X4),
-                        rhs_scale=wv_scales[:],
-                        start=True,
-                        stop=True,
+        def build_mixers(q):
+            b, g = divmod(q * QUAD, TENSOR_TILES)
+            mixer = mixers.tile([P, QUAD, H, T, NV], F32, name="mixer")
+            for t in range(T):
+                nc.gpsimd.tensor_scalar(
+                    out=mixer[:, :, :, t, :],
+                    in0=w_by_scene[:, b, g : g + QUAD, :, :],
+                    scalar1=same_t[:, t : t + 1],
+                    scalar2=0.0,
+                    op0=ALU.mult,
+                    op1=ALU.add,
+                )
+            mixer_of[q] = mixer
+
+        def project(pool, operand, first, weight):
+            codes, scales = operand
+            w_codes, w_scales = weight
+            tokens = slice(first, first + P)
+            sums = pool.tile([P, D], F32, name="sums")
+            nc.tensor.matmul_mx(
+                out=sums[:],
+                lhsT=codes[:, tokens].bitcast(FP8X4),
+                lhsT_scale=scales[:, tokens],
+                rhs=w_codes[:].bitcast(FP8X4),
+                rhs_scale=w_scales[:],
+                start=True,
+                stop=True,
+            )
+            return sums
+
+        n_tiles = B * TENSOR_TILES
+        v_of = {}
+        mixed_of = {}
+        grouped_of = {}
+        m_mx_of = {}
+        y_of = {}
+        y_sb_of = {}
+
+        def stage_v(n):
+            b, g = divmod(n, TENSOR_TILES)
+            v = project(ps_v, x_mx[(b, g // OCT)], (g % OCT) * P, wv_mx)
+            v_sb = three.tile([P, D], F32, name="v_sb")
+            nc.scalar.copy(out=v_sb[:], in_=v[:])
+            v_of[n] = v_sb
+
+        def stage_mix(n):
+            mixer = mixer_of[n // QUAD]
+            mix = ps_mix.tile([P, D], F32, name="mix")
+            for a in range(PACK):
+                nc.tensor.matmul(
+                    out=mix[:, a * P : (a + 1) * P],
+                    lhsT=bv_cols[:, a : a + 1].to_broadcast([P, P]),
+                    rhs=ident_f32[:],
+                    is_transpose=True,
+                    start=True,
+                    stop=False,
+                )
+                for h in range(2 * a, 2 * a + 2):
+                    head = slice(h * HD, (h + 1) * HD)
+                    nc.tensor.matmul(
+                        out=mix[:, head],
+                        lhsT=mixer[:, n % QUAD, h, :, :].rearrange("p t i -> p (t i)"),
+                        rhs=v_of[n][:, head],
+                        start=False,
+                        stop=(h == 2 * a + 1),
                     )
-                    for i in range(NV):
-                        for h in range(H):
-                            head = slice(h * HD, (h + 1) * HD)
-                            col = (h * B + b) * NV + i
-                            before = bv_all[:, head] if j == 0 else acc[:, i, head]
-                            after = mixed[:, i, head] if j == NV - 1 else acc[:, i, head]
-                            nc.vector.scalar_tensor_tensor(
-                                out=after,
-                                in0=v[:, head],
-                                scalar=w_cols[:, o, j, col : col + 1],
-                                in1=before,
-                                op0=ALU.mult,
-                                op1=ALU.add,
-                            )
+            mixed = three.tile([P, D], BF16, name="mixed")
+            nc.scalar.copy(out=mixed[:], in_=mix[:])
+            mixed_of[n] = mixed
+            if n % QUAD == 0 and n // QUAD + 2 < n_tiles // QUAD:
+                build_mixers(n // QUAD + 2)
 
-                mg = stream.tile([P, OCT * P * PACK], BF16, name="mg", align_bytes=64)
-                mg_tiles = mg[:].rearrange("p (r i t a) -> p r i t a", r=OCT, i=NV, t=T, a=PACK)
-                for i0 in range(0, NV, 2):
-                    mt = ps_mixed.tile([P, 2, PACK, P], BF16, name="mt")
-                    for k in range(2):
-                        for a in range(PACK):
-                            nc.tensor.transpose(
-                                out=mt[:, k, a, :],
-                                in_=mixed[:, i0 + k, a * P : (a + 1) * P],
-                                identity=ident_bf16[:],
-                            )
-                    for k in range(2):
-                        nc.scalar.copy(
-                            out=mg_tiles[:, :, i0 + k, :, :],
-                            in_=mt[:, k, :, :].rearrange("p a (r t) -> p r t a", r=OCT, t=T),
-                        )
-                m_codes = stream.tile([P, OCT * P], U32, name="m_codes", align_bytes=64)
-                m_scales = stream.tile([P, OCT * P], U8, name="m_scales", align_bytes=64)
-                nc.vector.quantize_mx(out=m_codes[:].bitcast(FP8X4), scales=m_scales[:], in_=mg[:])
+        def turn(mixed_rows):
+            mt = ps_turn.tile([P, PACK, P], BF16, tag="turn", name="mt")
+            for a in range(PACK):
+                nc.tensor.transpose(
+                    out=mt[:, a, :], in_=mixed_rows[:, a * P : (a + 1) * P], identity=ident_bf16[:]
+                )
+            return mt
 
-                for r0 in range(0, OCT, STORE):
-                    y_sb = results.tile([P, STORE, D], F32, name="y_sb")
-                    for k in range(STORE):
-                        tokens = slice((r0 + k) * P, (r0 + k + 1) * P)
-                        y = ps_y.tile([P, D], F32, name="y")
-                        nc.tensor.matmul_mx(
-                            out=y[:],
-                            lhsT=m_codes[:, tokens].bitcast(FP8X4),
-                            lhsT_scale=m_scales[:, tokens],
-                            rhs=wo_codes[:].bitcast(FP8X4),
-                            rhs_scale=wo_scales[:],
-                            start=True,
-                            stop=True,
-                        )
-                        nc.vector.tensor_tensor(out=y_sb[:, k, :], in0=y[:], in1=bo_all[:], op=ALU.add)
-                    g0 = o * OCT + r0
-                    nc.sync.dma_start(out=out_tiles[b, :, g0 : g0 + STORE, :], in_=y_sb[:])
+        def stage_turn(n):
+            mt = turn(mixed_of[n][:])
+            grouped = four.tile([P, NV, T, PACK], BF16, name="grouped", align_bytes=64)
+            nc.scalar.copy(out=grouped[:], in_=mt[:].rearrange("p a (t i) -> p i t a", t=T, i=NV))
+            grouped_of[n] = grouped
+
+        def stage_quantise(n):
+            codes = three.tile([P, P], U32, name="m_codes", align_bytes=64)
+            scales = three.tile([P, P], U8, name="m_scales", align_bytes=64)
+            nc.vector.quantize_mx(
+                out=codes[:].bitcast(FP8X4),
+                scales=scales[:],
+                in_=grouped_of[n][:].rearrange("p i t a -> p (i t a)"),
+            )
+            m_mx_of[n] = (codes, scales)
+
+        def add_bo_and_store(b, g, y):
+            if g % STORE == 0:
+                y_sb_of[(b, g // STORE)] = three.tile([P, STORE, D], F32, name="y_sb")
+            y_sb = y_sb_of[(b, g // STORE)]
+            nc.vector.tensor_tensor(out=y_sb[:, g % STORE, :], in0=y[:], in1=bo_all[:], op=ALU.add)
+            if g % STORE == STORE - 1:
+                nc.sync.dma_start(out=out_tiles[b, :, g - STORE + 1 : g + 1, :], in_=y_sb[:])
+
+        n_units = B * NV * NV
+        view_sums = {}
+        octet_sums = {}
+        octet_mixed = {}
+        octet_grouped = {}
+        octet_mx = {}
+
+        def project_view(n):
+            b, j = divmod(n, NV)
+            view_sums[n] = project(ps_view, x_mx[(b, VEC_OCT)], j * P, wv_mx)
+
+        def add_unit(u):
+            n, i = divmod(u, NV)
+            b, j = divmod(n, NV)
+            if i == UNITS and n + 1 < B * NV:
+                project_view(n + 1)
+            if i == 0 and j == 0:
+                octet_sums[b] = keep.tile([P, NV, D], F32, name="acc")
+            if i == 0 and j == NV - 1:
+                octet_mixed[b] = keep.tile([P, NV, D], BF16, name="mixed_v")
+            acc = octet_sums[b]
+            for h in range(H):
+                head = slice(h * HD, (h + 1) * HD)
+                col = (h * B + b) * NV + i
+                before = bv_all[:, head] if j == 0 else acc[:, i, head]
+                after = octet_mixed[b][:, i, head] if j == NV - 1 else acc[:, i, head]
+                nc.vector.scalar_tensor_tensor(
+                    out=after,
+                    in0=view_sums[n][:, head],
+                    scalar=w_cols[:, j, col : col + 1],
+                    in1=before,
+                    op0=ALU.mult,
+                    op1=ALU.add,
+                )
+
+        def turn_query_view(b, i):
+            if i == 0:
+                octet_grouped[b] = keep.tile([P, OCT, NV, T, PACK], BF16, name="mgv", align_bytes=64)
+            mt = turn(octet_mixed[b][:, i, :])
+            nc.scalar.copy(
+                out=octet_grouped[b][:, :, i, :, :], in_=mt[:].rearrange("p a (r t) -> p r t a", r=OCT, t=T)
+            )
+
+        def quantise_octet(b):
+            codes = keep.tile([P, OCT * P], U32, name="mv_codes", align_bytes=64)
+            scales = keep.tile([P, OCT * P], U8, name="mv_scales", align_bytes=64)
+            nc.vector.quantize_mx(
+                out=codes[:].bitcast(FP8X4),
+                scales=scales[:],
+                in_=octet_grouped[b][:].rearrange("p r i t a -> p (r i t a)"),
+            )
+            octet_mx[b] = (codes, scales)
+
+        load_x(0)
+        load_x(1)
+        wv_mx = quantise_weight(nc, setup, keep, "wv", load_wv)
+        raw_scores = load_scores(nc, setup, scores)
+        bv_all = keep.tile([P, D], BF16, name="bv_all")
+        nc.scalar.dma_start(out=bv_all[:], in_=bv.partition_broadcast(P))
+        bo_all = keep.tile([P, D], BF16, name="bo_all")
+        nc.scalar.dma_start(out=bo_all[:], in_=bo.partition_broadcast(P))
+        prepare_x(0)
+        exps = {}
+        for k in range(N_OCT + 1):
+            if k < N_OCT:
+                exps[k] = softmax_exponentials(nc, soft, raw_scores, octet_order[k])
+            if k > 0:
+                spread_weights(octet_order[k - 1], exps[k - 1])
+            if k == 1:
+                build_mixers(0)
+                build_mixers(1)
+                prepare_x(1)
+        bv_diag = setup.tile([P, PACK, P], F32, name="bv_diag")
+        nc.vector.tensor_tensor(
+            out=bv_diag[:],
+            in0=bv_all[:].rearrange("p (a c) -> p a c", a=PACK),
+            in1=ident_f32[:].unsqueeze(1).to_broadcast([P, PACK, P]),
+            op=ALU.mult,
+        )
+        bv_cols = keep.tile([P, PACK], F32, name="bv_cols")
+        nc.vector.tensor_reduce(out=bv_cols[:], in_=bv_diag[:], axis=mybir.AxisListType.X, op=ALU.add)
+        wo_mx = quantise_weight(nc, setup, keep, "wo", load_wo)
+        project_view(0)
+        for u in range(HEAD_START):
+            add_unit(u)
+        prepare_x(2)
+        prepare_x(3)
+
+        for count in range(n_tiles + 5):
+            s = count - 1
+            units = [u for u in range(HEAD_START + UNITS * count, HEAD_START + UNITS * (count + 1)) if u < n_units]
+            after = [count - 1 - (NV * NV * (b + 1) - 1 - HEAD_START) // UNITS for b in range(B)]
+
+            if 0 <= s - 4 < n_tiles:
+                y_of[s - 4] = project(ps_y, m_mx_of[s - 4], 0, wo_mx)
+            if 0 <= s + 1 < n_tiles:
+                stage_v(s + 1)
+            if 0 <= s - 4 < n_tiles:
+                add_bo_and_store((s - 4) // TENSOR_TILES, (s - 4) % TENSOR_TILES, y_of[s - 4])
+            if 0 <= s - 3 < n_tiles:
+                stage_quantise(s - 3)
+            for b in range(B):
+                if after[b] == 5:
+                    quantise_octet(b)
+            if 0 <= s < n_tiles:
+                stage_mix(s)
+            for u in units:
+                add_unit(u)
+            if 0 <= s - 1 < n_tiles:
+                stage_turn(s - 1)
+            for b in range(B):
+                if 0 <= after[b] < NV // 2:
+                    turn_query_view(b, 2 * after[b])
+                    turn_query_view(b, 2 * after[b] + 1)
+                if 5 <= after[b] < 5 + OCT:
+                    r = after[b] - 5
+                    y = project(ps_y, octet_mx[b], r * P, wo_mx)
+                    add_bo_and_store(b, TENSOR_TILES + r, y)
+            if count % 4 == 3 and count < 16:
+                prepare_x(len(x_order) // 2 + count // 4)

@@ -23,12 +23,11 @@ T = P // NV
 G = S // T
 OCT = 8
 N_OCT = G // OCT
-VEC_OCT = N_OCT - 1
-TENSOR_TILES = VEC_OCT * OCT
+TENSOR_OCTS = 2
+TENSOR_TILES = TENSOR_OCTS * OCT
+VECTOR_OCTS = N_OCT - TENSOR_OCTS
 QUAD = 4
 STORE = 2
-UNITS = 3
-HEAD_START = NV
 
 FLOPS = 2 * 2 * B * NV * S * D * D + 2 * B * NV * NV * S * D
 
@@ -100,8 +99,8 @@ def tile_crossviewattention_pa_t_kernel(tc, x, scores, Wv, bv, Wo, bo, out):
         four = stack.enter_context(tc.tile_pool(name="four", bufs=4))
         ps_view = stack.enter_context(tc.psum_pool(name="ps_view", bufs=2))
         ps_v = stack.enter_context(tc.psum_pool(name="ps_v", bufs=1))
-        ps_mix = stack.enter_context(tc.psum_pool(name="ps_mix", bufs=2))
-        ps_y = stack.enter_context(tc.psum_pool(name="ps_y", bufs=1))
+        ps_mix = stack.enter_context(tc.psum_pool(name="ps_mix", bufs=1))
+        ps_y = stack.enter_context(tc.psum_pool(name="ps_y", bufs=2))
         ps_turn = stack.enter_context(tc.psum_pool(name="ps_turn", bufs=2))
         stack.enter_context(tc.manual_schedule())
 
@@ -117,8 +116,8 @@ def tile_crossviewattention_pa_t_kernel(tc, x, scores, Wv, bv, Wo, bo, out):
             op=ALU.add,
         )
 
-        octet_order = [0, VEC_OCT] + list(range(1, VEC_OCT))
-        x_order = [(b, o) for b in range(B) for o in octet_order]
+        octet_order = [o + k for k in range(TENSOR_OCTS) for o in (0, TENSOR_OCTS)]
+        x_order = [(b, o) for b in range(B) for k in range(TENSOR_OCTS) for o in (TENSOR_OCTS + k, k)]
         x_loaded = {}
         x_mx = {}
 
@@ -146,7 +145,7 @@ def tile_crossviewattention_pa_t_kernel(tc, x, scores, Wv, bv, Wo, bo, out):
                         nc.tensor.transpose(
                             out=xt[:, k, u, :], in_=x_words[:, first : first + P], identity=ident_f32[:]
                         )
-                if o == VEC_OCT:
+                if o >= TENSOR_OCTS:
                     for k in range(2):
                         nc.scalar.copy(
                             out=by_view[:, :, r0 + k, :, :],
@@ -156,10 +155,9 @@ def tile_crossviewattention_pa_t_kernel(tc, x, scores, Wv, bv, Wo, bo, out):
                     nc.scalar.copy(
                         out=by_tile[:, r0 : r0 + 2, :, :], in_=xt[:].rearrange("p k u n -> p k n u")
                     )
-            pool = two if o == VEC_OCT else four
-            kind = "view" if o == VEC_OCT else "tile"
-            codes = pool.tile([P, OCT * P], U32, name="x_codes_" + kind, align_bytes=64)
-            scales = pool.tile([P, OCT * P], U8, name="x_scales_" + kind, align_bytes=64)
+            kind = "view" if o >= TENSOR_OCTS else "tile"
+            codes = two.tile([P, OCT * P], U32, name="x_codes_" + kind, align_bytes=64)
+            scales = two.tile([P, OCT * P], U8, name="x_scales_" + kind, align_bytes=64)
             nc.vector.quantize_mx(out=codes[:].bitcast(FP8X4), scales=scales[:], in_=xg[:])
             x_mx[(b, o)] = (codes, scales)
             if n + 2 < len(x_order):
@@ -176,13 +174,13 @@ def tile_crossviewattention_pa_t_kernel(tc, x, scores, Wv, bv, Wo, bo, out):
             nc.scalar.dma_start(out=raw[:], in_=Wo.rearrange("(a p) c -> p a c", p=P))
 
         w_rows = keep.tile([P, TENSOR_TILES, P], F32, name="w_rows")
-        w_cols = keep.tile([P, NV, P], F32, name="w_cols")
+        w_cols = keep.tile([P, VECTOR_OCTS, NV, P], F32, name="w_cols")
         w_by_scene = w_rows[:].rearrange("p g (h b i) -> p b g h i", h=H, b=B, i=NV)
 
         def spread_weights(o, e):
-            if o == VEC_OCT:
+            if o >= TENSOR_OCTS:
                 w = softmax_weights(nc, soft, e, "j r t", [NV, OCT, T])
-                turned = w_cols
+                turned = w_cols[:, o - TENSOR_OCTS, :, :]
             else:
                 w = softmax_weights(nc, soft, e, "r j t", [OCT, NV, T])
                 turned = w_rows[:, o * OCT : (o + 1) * OCT, :]
@@ -196,22 +194,22 @@ def tile_crossviewattention_pa_t_kernel(tc, x, scores, Wv, bv, Wo, bo, out):
                     )
                 nc.scalar.copy(out=turned[:, first : first + 4, :], in_=wt[:])
 
-        mixers = stack.enter_context(tc.tile_pool(name="mixers", bufs=3))
+        mixers = stack.enter_context(tc.tile_pool(name="mixers", bufs=2))
         mixer_of = {}
 
-        def build_mixers(q):
+        def build_mixers(q, columns):
             b, g = divmod(q * QUAD, TENSOR_TILES)
-            mixer = mixers.tile([P, QUAD, H, T, NV], F32, name="mixer")
-            for t in range(T):
+            if q not in mixer_of:
+                mixer_of[q] = mixers.tile([P, QUAD, H, T, NV], F32, name="mixer")
+            for t in columns:
                 nc.gpsimd.tensor_scalar(
-                    out=mixer[:, :, :, t, :],
+                    out=mixer_of[q][:, :, :, t, :],
                     in0=w_by_scene[:, b, g : g + QUAD, :, :],
                     scalar1=same_t[:, t : t + 1],
                     scalar2=0.0,
                     op0=ALU.mult,
                     op1=ALU.add,
                 )
-            mixer_of[q] = mixer
 
         def project(pool, operand, first, weight):
             codes, scales = operand
@@ -234,7 +232,6 @@ def tile_crossviewattention_pa_t_kernel(tc, x, scores, Wv, bv, Wo, bo, out):
         mixed_of = {}
         grouped_of = {}
         m_mx_of = {}
-        y_of = {}
         y_sb_of = {}
 
         def stage_v(n):
@@ -242,34 +239,23 @@ def tile_crossviewattention_pa_t_kernel(tc, x, scores, Wv, bv, Wo, bo, out):
             v = project(ps_v, x_mx[(b, g // OCT)], (g % OCT) * P, wv_mx)
             v_sb = three.tile([P, D], F32, name="v_sb")
             nc.scalar.copy(out=v_sb[:], in_=v[:])
+            nc.gpsimd.tensor_tensor(out=v_sb[:], in0=v_sb[:], in1=bv_all[:], op=ALU.add)
             v_of[n] = v_sb
 
         def stage_mix(n):
-            mixer = mixer_of[n // QUAD]
             mix = ps_mix.tile([P, D], F32, name="mix")
-            for a in range(PACK):
+            for h in range(H):
+                head = slice(h * HD, (h + 1) * HD)
                 nc.tensor.matmul(
-                    out=mix[:, a * P : (a + 1) * P],
-                    lhsT=bv_cols[:, a : a + 1].to_broadcast([P, P]),
-                    rhs=ident_f32[:],
-                    is_transpose=True,
+                    out=mix[:, head],
+                    lhsT=mixer_of[n // QUAD][:, n % QUAD, h, :, :].rearrange("p t i -> p (t i)"),
+                    rhs=v_of[n][:, head],
                     start=True,
-                    stop=False,
+                    stop=True,
                 )
-                for h in range(2 * a, 2 * a + 2):
-                    head = slice(h * HD, (h + 1) * HD)
-                    nc.tensor.matmul(
-                        out=mix[:, head],
-                        lhsT=mixer[:, n % QUAD, h, :, :].rearrange("p t i -> p (t i)"),
-                        rhs=v_of[n][:, head],
-                        start=False,
-                        stop=(h == 2 * a + 1),
-                    )
             mixed = three.tile([P, D], BF16, name="mixed")
             nc.scalar.copy(out=mixed[:], in_=mix[:])
             mixed_of[n] = mixed
-            if n % QUAD == 0 and n // QUAD + 2 < n_tiles // QUAD:
-                build_mixers(n // QUAD + 2)
 
         def turn(mixed_rows):
             mt = ps_turn.tile([P, PACK, P], BF16, tag="turn", name="mt")
@@ -295,66 +281,70 @@ def tile_crossviewattention_pa_t_kernel(tc, x, scores, Wv, bv, Wo, bo, out):
             )
             m_mx_of[n] = (codes, scales)
 
-        def add_bo_and_store(b, g, y):
+        def finish_tile(b, g, operand, first):
+            y = project(ps_y, operand, first, wo_mx)
             if g % STORE == 0:
                 y_sb_of[(b, g // STORE)] = three.tile([P, STORE, D], F32, name="y_sb")
             y_sb = y_sb_of[(b, g // STORE)]
-            nc.vector.tensor_tensor(out=y_sb[:, g % STORE, :], in0=y[:], in1=bo_all[:], op=ALU.add)
+            nc.scalar.copy(out=y_sb[:, g % STORE, :], in_=y[:])
+            nc.gpsimd.tensor_tensor(
+                out=y_sb[:, g % STORE, :], in0=y_sb[:, g % STORE, :], in1=bo_all[:], op=ALU.add
+            )
             if g % STORE == STORE - 1:
                 nc.sync.dma_start(out=out_tiles[b, :, g - STORE + 1 : g + 1, :], in_=y_sb[:])
 
-        n_units = B * NV * NV
+        n_pairs = B * VECTOR_OCTS * NV
         view_sums = {}
         octet_sums = {}
         octet_mixed = {}
         octet_grouped = {}
         octet_mx = {}
 
-        def project_view(n):
-            b, j = divmod(n, NV)
-            view_sums[n] = project(ps_view, x_mx[(b, VEC_OCT)], j * P, wv_mx)
+        def project_view(k):
+            m, j = divmod(k, NV)
+            octet = (m // VECTOR_OCTS, TENSOR_OCTS + m % VECTOR_OCTS)
+            view_sums[k] = project(ps_view, x_mx[octet], j * P, wv_mx)
 
-        def add_unit(u):
-            n, i = divmod(u, NV)
-            b, j = divmod(n, NV)
-            if i == UNITS and n + 1 < B * NV:
-                project_view(n + 1)
-            if i == 0 and j == 0:
-                octet_sums[b] = keep.tile([P, NV, D], F32, name="acc")
-            if i == 0 and j == NV - 1:
-                octet_mixed[b] = keep.tile([P, NV, D], BF16, name="mixed_v")
-            acc = octet_sums[b]
-            for h in range(H):
-                head = slice(h * HD, (h + 1) * HD)
-                col = (h * B + b) * NV + i
-                before = bv_all[:, head] if j == 0 else acc[:, i, head]
-                after = octet_mixed[b][:, i, head] if j == NV - 1 else acc[:, i, head]
-                nc.vector.scalar_tensor_tensor(
-                    out=after,
-                    in0=view_sums[n][:, head],
-                    scalar=w_cols[:, j, col : col + 1],
-                    in1=before,
-                    op0=ALU.mult,
-                    op1=ALU.add,
-                )
+        def add_view(k):
+            m, j = divmod(k, NV)
+            b = m // VECTOR_OCTS
+            if j == 0:
+                octet_sums[m] = keep.tile([P, NV, D], F32, name="acc")
+            if j == NV - 1:
+                octet_mixed[m] = keep.tile([P, NV, D], BF16, name="mixed_v")
+            acc = octet_sums[m]
+            for i in range(NV):
+                for h in range(H):
+                    head = slice(h * HD, (h + 1) * HD)
+                    col = (h * B + b) * NV + i
+                    before = bv_all[:, head] if j == 0 else acc[:, i, head]
+                    after = octet_mixed[m][:, i, head] if j == NV - 1 else acc[:, i, head]
+                    nc.vector.scalar_tensor_tensor(
+                        out=after,
+                        in0=view_sums[k][:, head],
+                        scalar=w_cols[:, m % VECTOR_OCTS, j, col : col + 1],
+                        in1=before,
+                        op0=ALU.mult,
+                        op1=ALU.add,
+                    )
 
-        def turn_query_view(b, i):
+        def turn_query_view(m, i):
             if i == 0:
-                octet_grouped[b] = keep.tile([P, OCT, NV, T, PACK], BF16, name="mgv", align_bytes=64)
-            mt = turn(octet_mixed[b][:, i, :])
+                octet_grouped[m] = keep.tile([P, OCT, NV, T, PACK], BF16, name="mgv", align_bytes=64)
+            mt = turn(octet_mixed[m][:, i, :])
             nc.scalar.copy(
-                out=octet_grouped[b][:, :, i, :, :], in_=mt[:].rearrange("p a (r t) -> p r t a", r=OCT, t=T)
+                out=octet_grouped[m][:, :, i, :, :], in_=mt[:].rearrange("p a (r t) -> p r t a", r=OCT, t=T)
             )
 
-        def quantise_octet(b):
+        def quantise_octet(m):
             codes = keep.tile([P, OCT * P], U32, name="mv_codes", align_bytes=64)
             scales = keep.tile([P, OCT * P], U8, name="mv_scales", align_bytes=64)
             nc.vector.quantize_mx(
                 out=codes[:].bitcast(FP8X4),
                 scales=scales[:],
-                in_=octet_grouped[b][:].rearrange("p r i t a -> p (r i t a)"),
+                in_=octet_grouped[m][:].rearrange("p r i t a -> p (r i t a)"),
             )
-            octet_mx[b] = (codes, scales)
+            octet_mx[m] = (codes, scales)
 
         load_x(0)
         load_x(1)
@@ -372,54 +362,42 @@ def tile_crossviewattention_pa_t_kernel(tc, x, scores, Wv, bv, Wo, bo, out):
             if k > 0:
                 spread_weights(octet_order[k - 1], exps[k - 1])
             if k == 1:
-                build_mixers(0)
-                build_mixers(1)
+                build_mixers(0, range(T))
                 prepare_x(1)
-        bv_diag = setup.tile([P, PACK, P], F32, name="bv_diag")
-        nc.vector.tensor_tensor(
-            out=bv_diag[:],
-            in0=bv_all[:].rearrange("p (a c) -> p a c", a=PACK),
-            in1=ident_f32[:].unsqueeze(1).to_broadcast([P, PACK, P]),
-            op=ALU.mult,
-        )
-        bv_cols = keep.tile([P, PACK], F32, name="bv_cols")
-        nc.vector.tensor_reduce(out=bv_cols[:], in_=bv_diag[:], axis=mybir.AxisListType.X, op=ALU.add)
         wo_mx = quantise_weight(nc, setup, keep, "wo", load_wo)
         project_view(0)
-        for u in range(HEAD_START):
-            add_unit(u)
-        prepare_x(2)
-        prepare_x(3)
+        project_view(1)
+        add_view(0)
 
-        for count in range(n_tiles + 5):
+        for count in range(n_pairs + NV - 1):
             s = count - 1
-            units = [u for u in range(HEAD_START + UNITS * count, HEAD_START + UNITS * (count + 1)) if u < n_units]
-            after = [count - 1 - (NV * NV * (b + 1) - 1 - HEAD_START) // UNITS for b in range(B)]
-
             if 0 <= s - 4 < n_tiles:
-                y_of[s - 4] = project(ps_y, m_mx_of[s - 4], 0, wo_mx)
+                finish_tile((s - 4) // TENSOR_TILES, (s - 4) % TENSOR_TILES, m_mx_of[s - 4], 0)
             if 0 <= s + 1 < n_tiles:
                 stage_v(s + 1)
-            if 0 <= s - 4 < n_tiles:
-                add_bo_and_store((s - 4) // TENSOR_TILES, (s - 4) % TENSOR_TILES, y_of[s - 4])
             if 0 <= s - 3 < n_tiles:
                 stage_quantise(s - 3)
-            for b in range(B):
-                if after[b] == 5:
-                    quantise_octet(b)
+            if 0 <= s < n_tiles - QUAD:
+                build_mixers(s // QUAD + 1, range(s % QUAD * QUAD, (s % QUAD + 1) * QUAD))
             if 0 <= s < n_tiles:
                 stage_mix(s)
-            for u in units:
-                add_unit(u)
+            if count + 2 < n_pairs:
+                project_view(count + 2)
+            since = [count - (NV * m + NV - 1) for m in range(B * VECTOR_OCTS)]
+            for m in range(B * VECTOR_OCTS):
+                if since[m] == NV // 2:
+                    quantise_octet(m)
+            if count + 1 < n_pairs:
+                add_view(count + 1)
             if 0 <= s - 1 < n_tiles:
                 stage_turn(s - 1)
-            for b in range(B):
-                if 0 <= after[b] < NV // 2:
-                    turn_query_view(b, 2 * after[b])
-                    turn_query_view(b, 2 * after[b] + 1)
-                if 5 <= after[b] < 5 + OCT:
-                    r = after[b] - 5
-                    y = project(ps_y, octet_mx[b], r * P, wo_mx)
-                    add_bo_and_store(b, TENSOR_TILES + r, y)
-            if count % 4 == 3 and count < 16:
-                prepare_x(len(x_order) // 2 + count // 4)
+            for m in range(B * VECTOR_OCTS):
+                for k in range(2):
+                    if 0 <= since[m] < NV // 2:
+                        turn_query_view(m, 2 * since[m] + k)
+                    if NV // 2 <= since[m] < NV:
+                        r = 2 * (since[m] - NV // 2) + k
+                        g = (TENSOR_OCTS + m % VECTOR_OCTS) * OCT + r
+                        finish_tile(m // VECTOR_OCTS, g, octet_mx[m], r * P)
+            if count % 4 == 1 and 2 + count // 4 < len(x_order):
+                prepare_x(2 + count // 4)

@@ -26,7 +26,7 @@ N_OCT = G // OCT
 TENSOR_OCTS = 2
 TENSOR_TILES = TENSOR_OCTS * OCT
 VECTOR_OCTS = N_OCT - TENSOR_OCTS
-QUAD = 4
+LEAD = 3
 STORE = 2
 
 FLOPS = 2 * 2 * B * NV * S * D * D + 2 * B * NV * NV * S * D
@@ -108,13 +108,15 @@ def tile_crossviewattention_pa_t_kernel(tc, x, scores, Wv, bv, Wo, bo, out):
         make_identity(nc, ident_f32[:])
         ident_bf16 = keep.tile([P, P], BF16, name="ident_bf16")
         make_identity(nc, ident_bf16[:])
-        same_t = keep.tile([P, T], F32, name="same_t")
+        same_t_once = keep.tile([P, T], F32, name="same_t_once")
         nc.vector.tensor_reduce(
-            out=same_t[:],
+            out=same_t_once[:],
             in_=ident_f32[:].rearrange("p (j t) -> p t j", j=NV, t=T),
             axis=mybir.AxisListType.X,
             op=ALU.add,
         )
+        same_t = keep.tile([P, T, NV], F32, name="same_t")
+        nc.vector.tensor_copy(out=same_t[:], in_=same_t_once[:].unsqueeze(2).to_broadcast([P, T, NV]))
 
         octet_order = [o + k for k in range(TENSOR_OCTS) for o in (0, TENSOR_OCTS)]
         x_order = [(b, o) for b in range(B) for k in range(TENSOR_OCTS) for o in (TENSOR_OCTS + k, k)]
@@ -194,22 +196,19 @@ def tile_crossviewattention_pa_t_kernel(tc, x, scores, Wv, bv, Wo, bo, out):
                     )
                 nc.scalar.copy(out=turned[:, first : first + 4, :], in_=wt[:])
 
-        mixers = stack.enter_context(tc.tile_pool(name="mixers", bufs=2))
+        mixers = stack.enter_context(tc.tile_pool(name="mixers", bufs=LEAD + 2))
         mixer_of = {}
 
-        def build_mixers(q, columns):
-            b, g = divmod(q * QUAD, TENSOR_TILES)
-            if q not in mixer_of:
-                mixer_of[q] = mixers.tile([P, QUAD, H, T, NV], F32, name="mixer")
-            for t in columns:
-                nc.gpsimd.tensor_scalar(
-                    out=mixer_of[q][:, :, :, t, :],
-                    in0=w_by_scene[:, b, g : g + QUAD, :, :],
-                    scalar1=same_t[:, t : t + 1],
-                    scalar2=0.0,
-                    op0=ALU.mult,
-                    op1=ALU.add,
-                )
+        def stage_mixers(n):
+            b, g = divmod(n, TENSOR_TILES)
+            mixer = mixers.tile([P, H, T, NV], F32, name="mixer")
+            nc.gpsimd.tensor_tensor(
+                out=mixer[:],
+                in0=w_by_scene[:, b, g, :, :].unsqueeze(2).to_broadcast([P, H, T, NV]),
+                in1=same_t[:].unsqueeze(1).to_broadcast([P, H, T, NV]),
+                op=ALU.mult,
+            )
+            mixer_of[n] = mixer
 
         def project(pool, operand, first, weight):
             codes, scales = operand
@@ -248,7 +247,7 @@ def tile_crossviewattention_pa_t_kernel(tc, x, scores, Wv, bv, Wo, bo, out):
                 head = slice(h * HD, (h + 1) * HD)
                 nc.tensor.matmul(
                     out=mix[:, head],
-                    lhsT=mixer_of[n // QUAD][:, n % QUAD, h, :, :].rearrange("p t i -> p (t i)"),
+                    lhsT=mixer_of[n][:, h, :, :].rearrange("p t i -> p (t i)"),
                     rhs=v_of[n][:, head],
                     start=True,
                     stop=True,
@@ -362,7 +361,8 @@ def tile_crossviewattention_pa_t_kernel(tc, x, scores, Wv, bv, Wo, bo, out):
             if k > 0:
                 spread_weights(octet_order[k - 1], exps[k - 1])
             if k == 1:
-                build_mixers(0, range(T))
+                for n in range(LEAD):
+                    stage_mixers(n)
                 prepare_x(1)
         wo_mx = quantise_weight(nc, setup, keep, "wo", load_wo)
         project_view(0)
@@ -377,8 +377,8 @@ def tile_crossviewattention_pa_t_kernel(tc, x, scores, Wv, bv, Wo, bo, out):
                 stage_v(s + 1)
             if 0 <= s - 3 < n_tiles:
                 stage_quantise(s - 3)
-            if 0 <= s < n_tiles - QUAD:
-                build_mixers(s // QUAD + 1, range(s % QUAD * QUAD, (s % QUAD + 1) * QUAD))
+            if LEAD <= s + LEAD < n_tiles:
+                stage_mixers(s + LEAD)
             if 0 <= s < n_tiles:
                 stage_mix(s)
             if count + 2 < n_pairs:

@@ -26,7 +26,7 @@ N_OCT = G // OCT
 TENSOR_OCTS = 2
 TENSOR_TILES = TENSOR_OCTS * OCT
 VECTOR_OCTS = N_OCT - TENSOR_OCTS
-LEAD = 3
+LEAD = 4
 STORE = 2
 
 FLOPS = 2 * 2 * B * NV * S * D * D + 2 * B * NV * NV * S * D
@@ -48,7 +48,7 @@ def quantise_weight(nc, setup, keep, name, load_rows):
 def load_scores(nc, setup, scores):
     raw = setup.tile([P, NV, S], BF16, name="scores_raw")
     for h in range(H):
-        nc.scalar.dma_start(
+        nc.sync.dma_start(
             out=raw[h * B * NV : (h + 1) * B * NV, :, :],
             in_=scores[:, :, :, h, :].rearrange("b i j s -> (b i) j s"),
         )
@@ -95,14 +95,13 @@ def tile_crossviewattention_pa_t_kernel(tc, x, scores, Wv, bv, Wo, bo, out):
         setup = stack.enter_context(tc.tile_pool(name="setup", bufs=1))
         soft = stack.enter_context(tc.tile_pool(name="soft", bufs=2))
         two = stack.enter_context(tc.tile_pool(name="two", bufs=2))
-        three = stack.enter_context(tc.tile_pool(name="three", bufs=3))
-        four = stack.enter_context(tc.tile_pool(name="four", bufs=4))
+        flow = stack.enter_context(tc.tile_pool(name="flow", bufs=4))
+        waiting = stack.enter_context(tc.tile_pool(name="waiting", bufs=6))
         ps_view = stack.enter_context(tc.psum_pool(name="ps_view", bufs=2))
         ps_v = stack.enter_context(tc.psum_pool(name="ps_v", bufs=1))
         ps_mix = stack.enter_context(tc.psum_pool(name="ps_mix", bufs=1))
         ps_y = stack.enter_context(tc.psum_pool(name="ps_y", bufs=2))
         ps_turn = stack.enter_context(tc.psum_pool(name="ps_turn", bufs=2))
-        stack.enter_context(tc.manual_schedule())
 
         ident_f32 = keep.tile([P, P], F32, name="ident_f32")
         make_identity(nc, ident_f32[:])
@@ -236,7 +235,7 @@ def tile_crossviewattention_pa_t_kernel(tc, x, scores, Wv, bv, Wo, bo, out):
         def stage_v(n):
             b, g = divmod(n, TENSOR_TILES)
             v = project(ps_v, x_mx[(b, g // OCT)], (g % OCT) * P, wv_mx)
-            v_sb = three.tile([P, D], F32, name="v_sb")
+            v_sb = flow.tile([P, D], F32, name="v_sb")
             nc.scalar.copy(out=v_sb[:], in_=v[:])
             nc.gpsimd.tensor_tensor(out=v_sb[:], in0=v_sb[:], in1=bv_all[:], op=ALU.add)
             v_of[n] = v_sb
@@ -252,7 +251,7 @@ def tile_crossviewattention_pa_t_kernel(tc, x, scores, Wv, bv, Wo, bo, out):
                     start=True,
                     stop=True,
                 )
-            mixed = three.tile([P, D], BF16, name="mixed")
+            mixed = flow.tile([P, D], BF16, name="mixed")
             nc.scalar.copy(out=mixed[:], in_=mix[:])
             mixed_of[n] = mixed
 
@@ -266,13 +265,13 @@ def tile_crossviewattention_pa_t_kernel(tc, x, scores, Wv, bv, Wo, bo, out):
 
         def stage_turn(n):
             mt = turn(mixed_of[n][:])
-            grouped = four.tile([P, NV, T, PACK], BF16, name="grouped", align_bytes=64)
+            grouped = waiting.tile([P, NV, T, PACK], BF16, name="grouped", align_bytes=64)
             nc.scalar.copy(out=grouped[:], in_=mt[:].rearrange("p a (t i) -> p i t a", t=T, i=NV))
             grouped_of[n] = grouped
 
         def stage_quantise(n):
-            codes = three.tile([P, P], U32, name="m_codes", align_bytes=64)
-            scales = three.tile([P, P], U8, name="m_scales", align_bytes=64)
+            codes = flow.tile([P, P], U32, name="m_codes", align_bytes=64)
+            scales = flow.tile([P, P], U8, name="m_scales", align_bytes=64)
             nc.vector.quantize_mx(
                 out=codes[:].bitcast(FP8X4),
                 scales=scales[:],
@@ -283,14 +282,17 @@ def tile_crossviewattention_pa_t_kernel(tc, x, scores, Wv, bv, Wo, bo, out):
         def finish_tile(b, g, operand, first):
             y = project(ps_y, operand, first, wo_mx)
             if g % STORE == 0:
-                y_sb_of[(b, g // STORE)] = three.tile([P, STORE, D], F32, name="y_sb")
-            y_sb = y_sb_of[(b, g // STORE)]
-            nc.scalar.copy(out=y_sb[:, g % STORE, :], in_=y[:])
-            nc.gpsimd.tensor_tensor(
-                out=y_sb[:, g % STORE, :], in0=y_sb[:, g % STORE, :], in1=bo_all[:], op=ALU.add
-            )
+                y_sb_of[(b, g // STORE)] = flow.tile([P, STORE, D], F32, name="y_sb")
+            y_sb = y_sb_of[(b, g // STORE)][:, g % STORE, :]
+            if g < TENSOR_TILES:
+                nc.scalar.copy(out=y_sb, in_=y[:])
+                nc.gpsimd.tensor_tensor(out=y_sb, in0=y_sb, in1=bo_all[:], op=ALU.add)
+            else:
+                nc.vector.tensor_tensor(out=y_sb, in0=y[:], in1=bo_all[:], op=ALU.add)
             if g % STORE == STORE - 1:
-                nc.sync.dma_start(out=out_tiles[b, :, g - STORE + 1 : g + 1, :], in_=y_sb[:])
+                nc.sync.dma_start(
+                    out=out_tiles[b, :, g - STORE + 1 : g + 1, :], in_=y_sb_of[(b, g // STORE)][:]
+                )
 
         n_pairs = B * VECTOR_OCTS * NV
         view_sums = {}
@@ -345,10 +347,10 @@ def tile_crossviewattention_pa_t_kernel(tc, x, scores, Wv, bv, Wo, bo, out):
             )
             octet_mx[m] = (codes, scales)
 
+        raw_scores = load_scores(nc, setup, scores)
         load_x(0)
         load_x(1)
         wv_mx = quantise_weight(nc, setup, keep, "wv", load_wv)
-        raw_scores = load_scores(nc, setup, scores)
         bv_all = keep.tile([P, D], BF16, name="bv_all")
         nc.scalar.dma_start(out=bv_all[:], in_=bv.partition_broadcast(P))
         bo_all = keep.tile([P, D], BF16, name="bo_all")

@@ -102,6 +102,7 @@ def tile_crossviewattention_pa_t_kernel(tc, x, scores, Wv, bv, Wo, bo, out):
         ps_mix = stack.enter_context(tc.psum_pool(name="ps_mix", bufs=1))
         ps_y = stack.enter_context(tc.psum_pool(name="ps_y", bufs=2))
         ps_turn = stack.enter_context(tc.psum_pool(name="ps_turn", bufs=2))
+        stack.enter_context(tc.manual_schedule())
 
         ident_f32 = keep.tile([P, P], F32, name="ident_f32")
         make_identity(nc, ident_f32[:])

from contextlib import ExitStack

import concourse.mybir as mybir
from concourse.masks import make_identity

F32 = mybir.dt.float32
BF16 = mybir.dt.bfloat16
U32 = mybir.dt.uint32
U8 = mybir.dt.uint8
FP8X4 = mybir.dt.float8_e4m3fn_x4
ALU = mybir.AluOpType
ACT = mybir.ActivationFunctionType

P = 128
PACK = 4
B = 2
NV = 8
S = 512
D = 512
H = 8
HD = D // H
T = P // NV
G = S // T
OCT = 8
N_OCT = G // OCT
TENSOR_OCTS = 2
TENSOR_TILES = TENSOR_OCTS * OCT
VECTOR_OCTS = N_OCT - TENSOR_OCTS
LEAD = 4
STORE = 2

FLOPS = 2 * 2 * B * NV * S * D * D + 2 * B * NV * NV * S * D


def quantise_weight(nc, setup, keep, name, load_rows):
    raw = setup.tile([P, PACK, D], BF16, name="w_raw")
    load_rows(raw)
    grouped = setup.tile([P, D, PACK], BF16, name="w_grouped", align_bytes=64)
    nc.vector.tensor_copy(out=grouped[:], in_=raw[:].rearrange("p a c -> p c a"))
    codes = keep.tile([P, D], U32, name=name + "_codes", align_bytes=64)
    scales = keep.tile([P, D], U8, name=name + "_scales", align_bytes=64)
    nc.vector.quantize_mx(
        out=codes[:].bitcast(FP8X4), scales=scales[:], in_=grouped[:].rearrange("p c a -> p (c a)")
    )
    return codes, scales


def load_scores(nc, setup, scores):
    raw = setup.tile([P, NV, S], BF16, name="scores_raw")
    for h in range(H):
        nc.sync.dma_start(
            out=raw[h * B * NV : (h + 1) * B * NV, :, :],
            in_=scores[:, :, :, h, :].rearrange("b i j s -> (b i) j s"),
        )
    return raw


def softmax_exponentials(nc, soft, raw, o):
    part = raw[:].rearrange("p j (t o r) -> p o j t r", t=T, o=N_OCT, r=OCT)[:, o, :, :, :]
    top = soft.tile([P, NV // 2, T, OCT], BF16, name="top")
    nc.vector.tensor_max(out=top[:], in0=part[:, 0:4, :, :], in1=part[:, 4:8, :, :])
    nc.vector.tensor_max(out=top[:, 0:2, :, :], in0=top[:, 0:2, :, :], in1=top[:, 2:4, :, :])
    nc.vector.tensor_max(out=top[:, 0:1, :, :], in0=top[:, 0:1, :, :], in1=top[:, 1:2, :, :])
    e = soft.tile([P, NV, T, OCT], F32, name="e")
    nc.vector.tensor_tensor(
        out=e[:], in0=part, in1=top[:, 0:1, :, :].to_broadcast([P, NV, T, OCT]), op=ALU.subtract
    )
    nc.scalar.activation(out=e[:], in_=e[:], func=ACT.Exp)
    return e


def softmax_weights(nc, soft, e, order, shape):
    total = soft.tile([P, NV // 2, T, OCT], F32, name="total")
    nc.vector.tensor_add(out=total[:], in0=e[:, 0:4, :, :], in1=e[:, 4:8, :, :])
    nc.vector.tensor_add(out=total[:, 0:2, :, :], in0=total[:, 0:2, :, :], in1=total[:, 2:4, :, :])
    nc.vector.tensor_add(out=total[:, 0:1, :, :], in0=total[:, 0:1, :, :], in1=total[:, 1:2, :, :])
    nc.vector.reciprocal(out=total[:, 0:1, :, :], in_=total[:, 0:1, :, :])
    w = soft.tile([P] + shape, F32, name="w")
    nc.vector.tensor_tensor(
        out=w[:],
        in0=e[:].rearrange("p j t r -> p " + order),
        in1=total[:, 0:1, :, :].rearrange("p j t r -> p " + order).to_broadcast([P] + shape),
        op=ALU.mult,
    )
    return w


def tile_crossviewattention_pa_t_kernel(tc, x, scores, Wv, bv, Wo, bo, out):
    nc = tc.nc
    x_tiles = x.flatten_outer_dims().rearrange("(b p g) d -> b p g d", b=B, p=P, g=G)
    out_tiles = out.flatten_outer_dims().rearrange("(b p g) d -> b p g d", b=B, p=P, g=G)

    with ExitStack() as stack:
        keep = stack.enter_context(tc.tile_pool(name="keep", bufs=1))
        setup = stack.enter_context(tc.tile_pool(name="setup", bufs=1))
        soft = stack.enter_context(tc.tile_pool(name="soft", bufs=2))
        two = stack.enter_context(tc.tile_pool(name="two", bufs=2))
        flow = stack.enter_context(tc.tile_pool(name="flow", bufs=4))
        waiting = stack.enter_context(tc.tile_pool(name="waiting", bufs=6))
        ps_view = stack.enter_context(tc.psum_pool(name="ps_view", bufs=2))
        ps_v = stack.enter_context(tc.psum_pool(name="ps_v", bufs=1))
        ps_mix = stack.enter_context(tc.psum_pool(name="ps_mix", bufs=1))
        ps_y = stack.enter_context(tc.psum_pool(name="ps_y", bufs=2))
        ps_turn = stack.enter_context(tc.psum_pool(name="ps_turn", bufs=2))
        stack.enter_context(tc.manual_schedule())

        ident_f32 = keep.tile([P, P], F32, name="ident_f32")
        make_identity(nc, ident_f32[:])
        ident_bf16 = keep.tile([P, P], BF16, name="ident_bf16")
        make_identity(nc, ident_bf16[:])
        same_t_once = keep.tile([P, T], F32, name="same_t_once")
        nc.vector.tensor_reduce(
            out=same_t_once[:],
            in_=ident_f32[:].rearrange("p (j t) -> p t j", j=NV, t=T),
            axis=mybir.AxisListType.X,
            op=ALU.add,
        )
        same_t = keep.tile([P, T, NV], F32, name="same_t")
        nc.vector.tensor_copy(out=same_t[:], in_=same_t_once[:].unsqueeze(2).to_broadcast([P, T, NV]))

        octet_order = [o + k for k in range(TENSOR_OCTS) for o in (0, TENSOR_OCTS)]
        x_order = [(b, o) for b in range(B) for k in range(TENSOR_OCTS) for o in (TENSOR_OCTS + k, k)]
        x_loaded = {}
        x_mx = {}

        def load_x(n):
            b, o = x_order[n]
            x_oct = two.tile([P, OCT * D], BF16, name="x_oct")
            nc.sync.dma_start(
                out=x_oct[:],
                in_=x_tiles[b, :, o * OCT : (o + 1) * OCT, :].rearrange("p r d -> p (r d)"),
            )
            x_loaded[n] = x_oct

        def prepare_x(n):
            b, o = x_order[n]
            x_words = x_loaded[n][:].bitcast(F32)
            xg = keep.tile([P, OCT * P * PACK], BF16, name="xg", align_bytes=64)
            xg_words = xg[:].bitcast(F32)
            by_tile = xg_words.rearrange("p (r n u) -> p r n u", r=OCT, n=P, u=2)
            by_view = xg_words.rearrange("p (j r t u) -> p j r t u", j=NV, r=OCT, t=T, u=2)
            for r0 in range(0, OCT, 2):
                xt = ps_turn.tile([P, 2, 2, P], F32, tag="turn", name="xt")
                for k in range(2):
                    for u in range(2):
                        first = (r0 + k) * (D // 2) + u * P
                        nc.tensor.transpose(
                            out=xt[:, k, u, :], in_=x_words[:, first : first + P], identity=ident_f32[:]
                        )
                if o >= TENSOR_OCTS:
                    for k in range(2):
                        nc.scalar.copy(
                            out=by_view[:, :, r0 + k, :, :],
                            in_=xt[:, k, :, :].rearrange("p u (j t) -> p j t u", j=NV, t=T),
                        )
                else:
                    nc.scalar.copy(
                        out=by_tile[:, r0 : r0 + 2, :, :], in_=xt[:].rearrange("p k u n -> p k n u")
                    )
            kind = "view" if o >= TENSOR_OCTS else "tile"
            codes = two.tile([P, OCT * P], U32, name="x_codes_" + kind, align_bytes=64)
            scales = two.tile([P, OCT * P], U8, name="x_scales_" + kind, align_bytes=64)
            nc.vector.quantize_mx(out=codes[:].bitcast(FP8X4), scales=scales[:], in_=xg[:])
            x_mx[(b, o)] = (codes, scales)
            if n + 2 < len(x_order):
                load_x(n + 2)

        def load_wv(raw):
            for u in range(2):
                nc.scalar.dma_start(
                    out=raw[:, 2 * u : 2 * u + 2, :],
                    in_=Wv[256 * u : 256 * (u + 1), :].rearrange("(q e) c -> q e c", e=2),
                )

        def load_wo(raw):
            nc.scalar.dma_start(out=raw[:], in_=Wo.rearrange("(a p) c -> p a c", p=P))

        w_rows = keep.tile([P, TENSOR_TILES, P], F32, name="w_rows")
        w_cols = keep.tile([P, VECTOR_OCTS, NV, P], F32, name="w_cols")
        w_by_scene = w_rows[:].rearrange("p g (h b i) -> p b g h i", h=H, b=B, i=NV)

        def spread_weights(o, e):
            if o >= TENSOR_OCTS:
                w = softmax_weights(nc, soft, e, "j r t", [NV, OCT, T])
                turned = w_cols[:, o - TENSOR_OCTS, :, :]
            else:
                w = softmax_weights(nc, soft, e, "r j t", [OCT, NV, T])
                turned = w_rows[:, o * OCT : (o + 1) * OCT, :]
            for first in range(0, OCT, 4):
                wt = ps_turn.tile([P, 4, P], F32, tag="turn", name="wt")
                for k in range(4):
                    nc.tensor.transpose(
                        out=wt[:, k, :],
                        in_=w[:, first + k, :, :].rearrange("p m n -> p (m n)"),
                        identity=ident_f32[:],
                    )
                nc.scalar.copy(out=turned[:, first : first + 4, :], in_=wt[:])

        mixers = stack.enter_context(tc.tile_pool(name="mixers", bufs=LEAD + 2))
        mixer_of = {}

        def stage_mixers(n):
            b, g = divmod(n, TENSOR_TILES)
            mixer = mixers.tile([P, H, T, NV], F32, name="mixer")
            nc.gpsimd.tensor_tensor(
                out=mixer[:],
                in0=w_by_scene[:, b, g, :, :].unsqueeze(2).to_broadcast([P, H, T, NV]),
                in1=same_t[:].unsqueeze(1).to_broadcast([P, H, T, NV]),
                op=ALU.mult,
            )
            mixer_of[n] = mixer

        def project(pool, operand, first, weight):
            codes, scales = operand
            w_codes, w_scales = weight
            tokens = slice(first, first + P)
            sums = pool.tile([P, D], F32, name="sums")
            nc.tensor.matmul_mx(
                out=sums[:],
                lhsT=codes[:, tokens].bitcast(FP8X4),
                lhsT_scale=scales[:, tokens],
                rhs=w_codes[:].bitcast(FP8X4),
                rhs_scale=w_scales[:],
                start=True,
                stop=True,
            )
            return sums

        n_tiles = B * TENSOR_TILES
        v_of = {}
        mixed_of = {}
        grouped_of = {}
        m_mx_of = {}
        y_sb_of = {}

        def stage_v(n):
            b, g = divmod(n, TENSOR_TILES)
            v = project(ps_v, x_mx[(b, g // OCT)], (g % OCT) * P, wv_mx)
            v_sb = flow.tile([P, D], F32, name="v_sb")
            nc.scalar.copy(out=v_sb[:], in_=v[:])
            nc.gpsimd.tensor_tensor(out=v_sb[:], in0=v_sb[:], in1=bv_all[:], op=ALU.add)
            v_of[n] = v_sb

        def stage_mix(n):
            mix = ps_mix.tile([P, D], F32, name="mix")
            for h in range(H):
                head = slice(h * HD, (h + 1) * HD)
                nc.tensor.matmul(
                    out=mix[:, head],
                    lhsT=mixer_of[n][:, h, :, :].rearrange("p t i -> p (t i)"),
                    rhs=v_of[n][:, head],
                    start=True,
                    stop=True,
                )
            mixed = flow.tile([P, D], BF16, name="mixed")
            nc.scalar.copy(out=mixed[:], in_=mix[:])
            mixed_of[n] = mixed

        def turn(mixed_rows):
            mt = ps_turn.tile([P, PACK, P], BF16, tag="turn", name="mt")
            for a in range(PACK):
                nc.tensor.transpose(
                    out=mt[:, a, :], in_=mixed_rows[:, a * P : (a + 1) * P], identity=ident_bf16[:]
                )
            return mt

        def stage_turn(n):
            mt = turn(mixed_of[n][:])
            grouped = waiting.tile([P, NV, T, PACK], BF16, name="grouped", align_bytes=64)
            nc.scalar.copy(out=grouped[:], in_=mt[:].rearrange("p a (t i) -> p i t a", t=T, i=NV))
            grouped_of[n] = grouped

        def stage_quantise(n):
            codes = flow.tile([P, P], U32, name="m_codes", align_bytes=64)
            scales = flow.tile([P, P], U8, name="m_scales", align_bytes=64)
            nc.vector.quantize_mx(
                out=codes[:].bitcast(FP8X4),
                scales=scales[:],
                in_=grouped_of[n][:].rearrange("p i t a -> p (i t a)"),
            )
            m_mx_of[n] = (codes, scales)

        def finish_tile(b, g, operand, first):
            y = project(ps_y, operand, first, wo_mx)
            if g % STORE == 0:
                y_sb_of[(b, g // STORE)] = flow.tile([P, STORE, D], F32, name="y_sb")
            y_sb = y_sb_of[(b, g // STORE)][:, g % STORE, :]
            if g < TENSOR_TILES:
                nc.scalar.copy(out=y_sb, in_=y[:])
                nc.gpsimd.tensor_tensor(out=y_sb, in0=y_sb, in1=bo_all[:], op=ALU.add)
            else:
                nc.vector.tensor_tensor(out=y_sb, in0=y[:], in1=bo_all[:], op=ALU.add)
            if g % STORE == STORE - 1:
                nc.sync.dma_start(
                    out=out_tiles[b, :, g - STORE + 1 : g + 1, :], in_=y_sb_of[(b, g // STORE)][:]
                )

        n_pairs = B * VECTOR_OCTS * NV
        view_sums = {}
        octet_sums = {}
        octet_mixed = {}
        octet_grouped = {}
        octet_mx = {}

        def project_view(k):
            m, j = divmod(k, NV)
            octet = (m // VECTOR_OCTS, TENSOR_OCTS + m % VECTOR_OCTS)
            view_sums[k] = project(ps_view, x_mx[octet], j * P, wv_mx)

        def add_view(k):
            m, j = divmod(k, NV)
            b = m // VECTOR_OCTS
            if j == 0:
                octet_sums[m] = keep.tile([P, NV, D], F32, name="acc")
            if j == NV - 1:
                octet_mixed[m] = keep.tile([P, NV, D], BF16, name="mixed_v")
            acc = octet_sums[m]
            for i in range(NV):
                for h in range(H):
                    head = slice(h * HD, (h + 1) * HD)
                    col = (h * B + b) * NV + i
                    before = bv_all[:, head] if j == 0 else acc[:, i, head]
                    after = octet_mixed[m][:, i, head] if j == NV - 1 else acc[:, i, head]
                    nc.vector.scalar_tensor_tensor(
                        out=after,
                        in0=view_sums[k][:, head],
                        scalar=w_cols[:, m % VECTOR_OCTS, j, col : col + 1],
                        in1=before,
                        op0=ALU.mult,
                        op1=ALU.add,
                    )

        def turn_query_view(m, i):
            if i == 0:
                octet_grouped[m] = keep.tile([P, OCT, NV, T, PACK], BF16, name="mgv", align_bytes=64)
            mt = turn(octet_mixed[m][:, i, :])
            nc.scalar.copy(
                out=octet_grouped[m][:, :, i, :, :], in_=mt[:].rearrange("p a (r t) -> p r t a", r=OCT, t=T)
            )

        def quantise_octet(m):
            codes = keep.tile([P, OCT * P], U32, name="mv_codes", align_bytes=64)
            scales = keep.tile([P, OCT * P], U8, name="mv_scales", align_bytes=64)
            nc.vector.quantize_mx(
                out=codes[:].bitcast(FP8X4),
                scales=scales[:],
                in_=octet_grouped[m][:].rearrange("p r i t a -> p (r i t a)"),
            )
            octet_mx[m] = (codes, scales)

        raw_scores = load_scores(nc, setup, scores)
        load_x(0)
        load_x(1)
        wv_mx = quantise_weight(nc, setup, keep, "wv", load_wv)
        bv_all = keep.tile([P, D], BF16, name="bv_all")
        nc.scalar.dma_start(out=bv_all[:], in_=bv.partition_broadcast(P))
        bo_all = keep.tile([P, D], BF16, name="bo_all")
        nc.scalar.dma_start(out=bo_all[:], in_=bo.partition_broadcast(P))
        prepare_x(0)
        exps = {}
        for k in range(N_OCT + 1):
            if k < N_OCT:
                exps[k] = softmax_exponentials(nc, soft, raw_scores, octet_order[k])
            if k > 0:
                spread_weights(octet_order[k - 1], exps[k - 1])
            if k == 1:
                for n in range(LEAD):
                    stage_mixers(n)
                prepare_x(1)
        wo_mx = quantise_weight(nc, setup, keep, "wo", load_wo)
        project_view(0)
        project_view(1)
        add_view(0)

        for count in range(n_pairs + NV - 1):
            s = count - 1
            if 0 <= s - 4 < n_tiles:
                finish_tile((s - 4) // TENSOR_TILES, (s - 4) % TENSOR_TILES, m_mx_of[s - 4], 0)
            if 0 <= s + 1 < n_tiles:
                stage_v(s + 1)
            if 0 <= s - 3 < n_tiles:
                stage_quantise(s - 3)
            if LEAD <= s + LEAD < n_tiles:
                stage_mixers(s + LEAD)
            if 0 <= s < n_tiles:
                stage_mix(s)
            if count + 2 < n_pairs:
                project_view(count + 2)
            since = [count - (NV * m + NV - 1) for m in range(B * VECTOR_OCTS)]
            for m in range(B * VECTOR_OCTS):
                if since[m] == NV // 2:
                    quantise_octet(m)
            if count + 1 < n_pairs:
                add_view(count + 1)
            if 0 <= s - 1 < n_tiles:
                stage_turn(s - 1)
            for m in range(B * VECTOR_OCTS):
                for k in range(2):
                    if 0 <= since[m] < NV // 2:
                        turn_query_view(m, 2 * since[m] + k)
                    if NV // 2 <= since[m] < NV:
                        r = 2 * (since[m] - NV // 2) + k
                        g = (TENSOR_OCTS + m % VECTOR_OCTS) * OCT + r
                        finish_tile(m // VECTOR_OCTS, g, octet_mx[m], r * P)
            if count % 4 == 1 and 2 + count // 4 < len(x_order):
                prepare_x(2 + count // 4)
